import numpy as np
import ml_dtypes


def mxq(x, axis, fmt="e4m3"):
    dtype, down = {"e4m3": (ml_dtypes.float8_e4m3fn, 7), "e5m2": (ml_dtypes.float8_e5m2, 14)}[fmt]
    v = np.moveaxis(np.asarray(x, np.float32).astype(ml_dtypes.bfloat16).astype(np.float64), axis, -1)
    blocks = v.reshape(v.shape[:-1] + (-1, 32))
    amax = np.abs(blocks).max(-1, keepdims=True)
    byte = np.maximum(np.where(amax > 0, np.frexp(amax)[1] - 1 + 127, 0) - down, 1)
    scale = np.exp2(byte - 127.0)
    codes = (blocks / scale).astype(np.float32).astype(dtype).astype(np.float64)
    return np.moveaxis((codes * scale).reshape(v.shape), -1, axis)


WIDE = False


def mx_kscale(k):
    if not WIDE:
        return np.ones(k)
    levels = np.array([10, -10, 5, -5, 0])
    a = np.random.permutation(np.resize(levels, k // 512 * 4)).reshape(k // 512, 4)
    idx = np.arange(k)
    return np.exp2(a[idx // 512, idx % 128 // 32])


BF16 = ml_dtypes.bfloat16


def bf(x):
    return np.asarray(x, np.float32).astype(BF16)


def f64(x):
    return np.asarray(x).astype(np.float64)


B, IN_C, OUT_C, H, W, K, STRIDE, PAD = 128, 512, 128, 4, 4, 3, 1, 1
OH = (H + 2 * PAD - K) // STRIDE + 1
OW = (W + 2 * PAD - K) // STRIDE + 1


def _span(t, n_in, n_out):
    lo = max(0, -((t - PAD) // STRIDE))
    hi = min(n_out, (n_in - 1 + PAD - t) // STRIDE + 1)
    return lo, hi


def setup_inputs():
    s = mx_kscale(IN_C)
    x = np.random.standard_normal((B, IN_C, H, W)) * s[None, :, None, None]
    weights = np.random.uniform(0.0, 1.0, (OH, OW, OUT_C, IN_C, K, K)) * (1.7 / np.sqrt(IN_C * K * K)) / s[None, None, None, :, None, None]
    bias = np.random.uniform(0.0, 1.0, (OUT_C, OH, OW))
    return {"x": bf(x), "weights": bf(weights), "bias": bf(bias)}


def reference(x, weights, bias):
    xq = mxq(f64(x), 1, "e4m3")
    wf = f64(weights)
    acc = np.zeros((OH, OW, B, OUT_C))
    for i in range(K):
        h0, h1 = _span(i, H, OH)
        for j in range(K):
            w0, w1 = _span(j, W, OW)
            xs = xq[:, :, h0 * STRIDE + i - PAD:(h1 - 1) * STRIDE + i - PAD + 1:STRIDE,
                    w0 * STRIDE + j - PAD:(w1 - 1) * STRIDE + j - PAD + 1:STRIDE]
            wq = mxq(wf[h0:h1, w0:w1, :, :, i, j], 3, "e4m3")
            acc[h0:h1, w0:w1] += xs.transpose(2, 3, 0, 1) @ wq.transpose(0, 1, 3, 2)
    return acc.transpose(2, 3, 0, 1) + f64(bias)[None]

@@ -1,0 +1,246 @@
+from contextlib import ExitStack
+
+import concourse.mybir as mybir
+from concourse.masks import make_identity
+
+BF16 = mybir.dt.bfloat16
+F32 = mybir.dt.float32
+U32 = mybir.dt.uint32
+U8 = mybir.dt.uint8
+FP8X4 = mybir.dt.float8_e4m3fn_x4
+
+P = 128
+B = 128
+C = 512
+O = 128
+HW = 4
+KK = 3
+NPIX = HW * HW
+NTAP = KK * KK
+ROW = C * NTAP
+GROUP = 4
+FLOPS = 2 * 100 * B * O * C
+
+LOAD_BUFS = 9
+D_BUFS = 4
+G_BUFS = 3
+Q_BUFS = 4
+TP_BUFS = 6
+ACT_EVERY = 5
+MANUAL = False
+
+
+def valid(p):
+    return [t for t in range(KK) if 0 <= p + t - 1 < HW]
+
+
+def tile_locallyconnected2d_kernel(tc, x, weights, bias, out):
+    nc = tc.nc
+    with ExitStack() as ctx:
+        if MANUAL:
+            ctx.enter_context(tc.manual_schedule())
+        const = ctx.enter_context(tc.tile_pool(name="const", bufs=1))
+        loads = ctx.enter_context(tc.tile_pool(name="loads", bufs=LOAD_BUFS))
+        dpool = ctx.enter_context(tc.tile_pool(name="dpool", bufs=D_BUFS))
+        gpool = ctx.enter_context(tc.tile_pool(name="gpool", bufs=G_BUFS))
+        qpool = ctx.enter_context(tc.tile_pool(name="qpool", bufs=Q_BUFS))
+        tpool = ctx.enter_context(tc.psum_pool(name="tpool", bufs=TP_BUFS))
+        apool = ctx.enter_context(tc.psum_pool(name="apool", bufs=2))
+
+        locs = [(h, w) for h in range(HW) for w in range(HW)]
+
+        x_raw = []
+        for hf in range(2):
+            t = loads.tile([P, ROW], BF16, tag="ld", name="xraw%d" % hf)
+            nc.sync.dma_start(
+                out=t[:, 0 : 256 * NPIX],
+                in_=x[:, 256 * hf : 256 * (hf + 1)].rearrange("b c y x -> b (c y x)"),
+            )
+            x_raw.append(t)
+
+        ident = const.tile([P, P], F32, name="ident")
+        make_identity(nc, ident[:])
+        ones = const.tile([P, P], BF16, name="ones")
+        nc.vector.memset(ones[:], 1.0)
+        brow = const.tile([P, O * NPIX], BF16, name="brow")
+        nc.vector.memset(brow[:], 0.0)
+        nc.scalar.dma_start(out=brow[0:1, :], in_=bias.rearrange("(a o) y x -> a (o y x)", a=1))
+        bias_all = const.tile([P, O * NPIX], F32, name="bias_all")
+        result = const.tile([P, O * NPIX], F32, name="result")
+        xq = const.tile([P, NPIX * B], U32, name="xq", align_bytes=64)
+        xs = const.tile([P, NPIX * B], U8, name="xs", align_bytes=64)
+
+        w_raw = {}
+
+        def load_w(k):
+            h, w = locs[k]
+            t = loads.tile([P, ROW], BF16, tag="ld", name="wraw%d" % k)
+            nc.sync.dma_start(out=t[:], in_=weights[h, w].rearrange("o c i j -> o (c i j)"))
+            w_raw[k] = t
+
+        next_load = [0]
+
+        def load_next():
+            if next_load[0] < len(locs):
+                load_w(next_load[0])
+                next_load[0] += 1
+
+        for k in range(LOAD_BUFS - 2):
+            load_next()
+
+        counter = [0]
+
+        def deinterleave(dst, src):
+            counter[0] += 1
+            if counter[0] % ACT_EVERY == 0:
+                nc.scalar.copy(out=dst, in_=src)
+            else:
+                nc.vector.tensor_copy(out=dst, in_=src)
+
+        def transpose_pair(ps, slots):
+            for t in range(2):
+                d, s = slots[t]
+                for u in range(2):
+                    nc.tensor.transpose(
+                        ps[:, (2 * t + u) * P : (2 * t + u + 1) * P],
+                        d[:, s * 256 + u * P : s * 256 + (u + 1) * P],
+                        ident[:],
+                    )
+
+        def evacuate(engine_copy, g32, ps):
+            engine_copy(
+                out=g32.rearrange("p (t o u) -> p t o u", t=2, u=2),
+                in_=ps[:].rearrange("p (t u o) -> p t o u", t=2, u=2),
+            )
+
+        dxs = [dpool.tile([P, ROW], BF16, tag="d", name="dx%d" % pg) for pg in range(2)]
+        n_x = 0
+        for hf in range(2):
+            for pg in range(2):
+                for q4 in range(2):
+                    n_x += 1
+                    (nc.scalar.copy if n_x % 3 == 0 else nc.vector.tensor_copy)(
+                        out=dxs[pg][:, 0 : 8 * C].rearrange("b (s c) -> b c s", c=C)[
+                            :, 256 * hf : 256 * (hf + 1), 4 * q4 : 4 * q4 + 4
+                        ],
+                        in_=x_raw[hf][:, 0 : 256 * NPIX].rearrange("b (c s) -> b c s", s=NPIX)[
+                            :, :, 8 * pg + 4 * q4 : 8 * pg + 4 * q4 + 4
+                        ],
+                    )
+        load_next()
+        load_next()
+        for pg in range(2):
+            dx32 = dxs[pg][:].bitcast(F32)
+            for half in range(2):
+                g = gpool.tile([P, GROUP * C], BF16, tag="g", name="gx%d_%d" % (pg, half), align_bytes=64)
+                g32 = g[:].bitcast(F32)
+                for bk in range(2):
+                    ps = tpool.tile([P, 512], F32, tag="tp", name="px%d_%d_%d" % (pg, half, bk))
+                    s0 = 4 * half + 2 * bk
+                    transpose_pair(ps, [(dx32, s0), (dx32, s0 + 1)])
+                    evacuate(
+                        nc.scalar.copy if bk == 0 else nc.vector.tensor_copy,
+                        g32[:, 512 * bk : 512 * (bk + 1)],
+                        ps,
+                    )
+                p0 = (8 * pg + 4 * half) * B
+                nc.vector.quantize_mx(
+                    out=xq[:, p0 : p0 + GROUP * B].bitcast(FP8X4),
+                    scales=xs[:, p0 : p0 + GROUP * B],
+                    in_=g[:],
+                )
+
+        taps = []
+        for k, (h, w) in enumerate(locs):
+            lst = [(i, j) for i in valid(h) for j in valid(w)]
+            for s, (i, j) in enumerate(lst):
+                taps.append((k, h, w, i, j, s, s == 0, s == len(lst) - 1))
+        groups = [taps[a : a + GROUP] for a in range(0, len(taps), GROUP)]
+        ng = len(groups)
+
+        d32_of = {}
+
+        def s2(k):
+            h, w = locs[k]
+            js = valid(w)
+            nj = len(js)
+            d = dpool.tile([P, ROW], BF16, tag="d", name="d%d" % k)
+            src = w_raw[k][:].rearrange("o (c t) -> o c t", t=NTAP)
+            for a, i in enumerate(valid(h)):
+                deinterleave(
+                    d[:, a * nj * C : (a + 1) * nj * C].rearrange("o (s c) -> o c s", c=C),
+                    src[:, :, KK * i + js[0] : KK * i + js[0] + nj],
+                )
+            load_next()
+            d32_of[k] = d[:].bitcast(F32)
+
+        done_s2 = [0]
+
+        def ensure_s2(upto):
+            while done_s2[0] <= upto:
+                s2(done_s2[0])
+                done_s2[0] += 1
+
+        g_of = {}
+        q_of = {}
+        acc_of = {}
+
+        def stage_t(gi):
+            grp = groups[gi]
+            g = gpool.tile([P, GROUP * C], BF16, tag="g", name="g%d" % gi, align_bytes=64)
+            g32 = g[:].bitcast(F32)
+            for bk in range(2):
+                ps = tpool.tile([P, 512], F32, tag="tp", name="pw%d_%d" % (gi, bk))
+                ta, tb = grp[2 * bk], grp[2 * bk + 1]
+                transpose_pair(ps, [(d32_of[ta[0]], ta[5]), (d32_of[tb[0]], tb[5])])
+                evacuate(nc.scalar.copy, g32[:, 512 * bk : 512 * (bk + 1)], ps)
+            g_of[gi] = g
+
+        def stage_q(gi):
+            wq = qpool.tile([P, GROUP * O], U32, tag="wq", name="wq%d" % gi, align_bytes=64)
+            ws = qpool.tile([P, GROUP * O], U8, tag="ws", name="ws%d" % gi, align_bytes=64)
+            nc.vector.quantize_mx(out=wq[:].bitcast(FP8X4), scales=ws[:], in_=g_of[gi][:])
+            q_of[gi] = (wq, ws)
+
+        def stage_m(gi):
+            wq, ws = q_of[gi]
+            for n, (k, h, w, i, j, s, first, last) in enumerate(groups[gi]):
+                if w == 0 and first:
+                    acc_of[h] = apool.tile([P, 512], F32, tag="acc", name="acc%d" % h)
+                acc = acc_of[h]
+                pix = (h + i - 1) * HW + (w + j - 1)
+                nc.tensor.matmul_mx(
+                    out=acc[:, w * O : (w + 1) * O],
+                    lhsT=xq[:, pix * B : (pix + 1) * B].bitcast(FP8X4),
+                    lhsT_scale=xs[:, pix * B : (pix + 1) * B],
+                    rhs=wq[:, n * O : (n + 1) * O].bitcast(FP8X4),
+                    rhs_scale=ws[:, n * O : (n + 1) * O],
+                    start=first,
+                    stop=last,
+                )
+                if w == HW - 1 and last:
+                    nc.vector.tensor_tensor(
+                        out=result[:].rearrange("b (o l) -> b o l", l=NPIX)[:, :, HW * h : HW * (h + 1)],
+                        in0=acc[:].rearrange("b (w o) -> b o w", w=HW),
+                        in1=bias_all[:].rearrange("b (o l) -> b o l", l=NPIX)[:, :, HW * h : HW * (h + 1)],
+                        op=mybir.AluOpType.add,
+                    )
+
+        def bias_broadcast():
+            for k in range(4):
+                pb = tpool.tile([P, 512], F32, tag="tp", name="pb%d" % k)
+                nc.tensor.matmul(pb[:], lhsT=ones[:], rhs=brow[:, 512 * k : 512 * (k + 1)], start=True, stop=True)
+                nc.scalar.copy(out=bias_all[:, 512 * k : 512 * (k + 1)], in_=pb[:])
+
+        for s in range(ng + 2):
+            if s == 3:
+                bias_broadcast()
+            if s < ng:
+                ensure_s2(groups[min(s + 1, ng - 1)][-1][0])
+                stage_t(s)
+            if 1 <= s <= ng:
+                stage_q(s - 1)
+            if s >= 2:
+                stage_m(s - 2)
+
+        nc.sync.dma_start(out=out.rearrange("b o y x -> b (o y x)"), in_=result[:])

@@ -25,7 +25,8 @@ LOAD_BUFS = 9
 D_BUFS = 4
 G_BUFS = 3
 Q_BUFS = 4
-TP_BUFS = 6
+TP_BUFS = 5
+DUMMIES = 2
 ACT_EVERY = 5
 MANUAL = False
 
@@ -46,6 +47,8 @@ def tile_locallyconnected2d_kernel(tc, x, weights, bias, out):
         qpool = ctx.enter_context(tc.tile_pool(name="qpool", bufs=Q_BUFS))
         tpool = ctx.enter_context(tc.psum_pool(name="tpool", bufs=TP_BUFS))
         apool = ctx.enter_context(tc.psum_pool(name="apool", bufs=2))
+        spool = ctx.enter_context(tc.psum_pool(name="spool", bufs=1))
+        scratch = spool.tile([P, 512], F32, name="scratch")
 
         locs = [(h, w) for h in range(HW) for w in range(HW)]
 
@@ -204,6 +207,16 @@ def tile_locallyconnected2d_kernel(tc, x, weights, bias, out):
 
         def stage_m(gi):
             wq, ws = q_of[gi]
+            for n in range(DUMMIES):
+                nc.tensor.matmul_mx(
+                    out=scratch[:],
+                    lhsT=xq[:, 0:B].bitcast(FP8X4),
+                    lhsT_scale=xs[:, 0:B],
+                    rhs=wq[:].bitcast(FP8X4),
+                    rhs_scale=ws[:],
+                    start=True,
+                    stop=True,
+                )
             for n, (k, h, w, i, j, s, first, last) in enumerate(groups[gi]):
                 if w == 0 and first:
                     acc_of[h] = apool.tile([P, 512], F32, tag="acc", name="acc%d" % h)

@@ -22,13 +22,14 @@ GROUP = 4
 FLOPS = 2 * 100 * B * O * C
 
 LOAD_BUFS = 9
-D_BUFS = 4
+D_BUFS = 6
 G_BUFS = 3
 Q_BUFS = 4
 TP_BUFS = 5
 DUMMIES = 2
-ACT_EVERY = 5
-MANUAL = False
+EVAC_ACT_EVERY = 5
+LOOKAHEAD = 3
+MANUAL = True
 
 
 def valid(p):
@@ -91,14 +92,23 @@ def tile_locallyconnected2d_kernel(tc, x, weights, bias, out):
         for k in range(LOAD_BUFS - 2):
             load_next()
 
-        counter = [0]
+        load_est = [6.5, 13.1]
 
-        def deinterleave(dst, src):
-            counter[0] += 1
-            if counter[0] % ACT_EVERY == 0:
+        def deinterleave(dst, src, n_el):
+            if load_est[0] + 0.00095 * n_el <= load_est[1] + 0.00105 * n_el:
+                load_est[0] += 0.00095 * n_el
                 nc.scalar.copy(out=dst, in_=src)
             else:
-                nc.vector.tensor_copy(out=dst, in_=src)
+                load_est[1] += 0.00105 * n_el
+                nc.gpsimd.tensor_scalar(
+                    out=dst, in0=src, scalar1=1.0, scalar2=0.0, op0=mybir.AluOpType.mult, op1=mybir.AluOpType.add
+                )
+
+        n_evac = [0]
+
+        def evac_engine():
+            n_evac[0] += 1
+            return nc.scalar.copy if n_evac[0] % EVAC_ACT_EVERY == 0 else nc.vector.tensor_copy
 
         def transpose_pair(ps, slots):
             for t in range(2):
@@ -122,7 +132,7 @@ def tile_locallyconnected2d_kernel(tc, x, weights, bias, out):
             for pg in range(2):
                 for q4 in range(2):
                     n_x += 1
-                    (nc.scalar.copy if n_x % 3 == 0 else nc.vector.tensor_copy)(
+                    (nc.scalar.copy if n_x % 3 == 2 else nc.vector.tensor_copy)(
                         out=dxs[pg][:, 0 : 8 * C].rearrange("b (s c) -> b c s", c=C)[
                             :, 256 * hf : 256 * (hf + 1), 4 * q4 : 4 * q4 + 4
                         ],
@@ -132,6 +142,18 @@ def tile_locallyconnected2d_kernel(tc, x, weights, bias, out):
                     )
         load_next()
         load_next()
+        pending = []
+        n_xq = [0]
+
+        def quantise_x():
+            g, p0 = pending[n_xq[0]]
+            n_xq[0] += 1
+            nc.vector.quantize_mx(
+                out=xq[:, p0 : p0 + GROUP * B].bitcast(FP8X4),
+                scales=xs[:, p0 : p0 + GROUP * B],
+                in_=g[:],
+            )
+
         for pg in range(2):
             dx32 = dxs[pg][:].bitcast(F32)
             for half in range(2):
@@ -146,12 +168,10 @@ def tile_locallyconnected2d_kernel(tc, x, weights, bias, out):
                         g32[:, 512 * bk : 512 * (bk + 1)],
                         ps,
                     )
-                p0 = (8 * pg + 4 * half) * B
-                nc.vector.quantize_mx(
-                    out=xq[:, p0 : p0 + GROUP * B].bitcast(FP8X4),
-                    scales=xs[:, p0 : p0 + GROUP * B],
-                    in_=g[:],
-                )
+                pending.append((g, (8 * pg + 4 * half) * B))
+                if len(pending) > 1:
+                    quantise_x()
+        quantise_x()
 
         taps = []
         for k, (h, w) in enumerate(locs):
@@ -173,6 +193,7 @@ def tile_locallyconnected2d_kernel(tc, x, weights, bias, out):
                 deinterleave(
                     d[:, a * nj * C : (a + 1) * nj * C].rearrange("o (s c) -> o c s", c=C),
                     src[:, :, KK * i + js[0] : KK * i + js[0] + nj],
+                    nj * C,
                 )
             load_next()
             d32_of[k] = d[:].bitcast(F32)
@@ -196,7 +217,7 @@ def tile_locallyconnected2d_kernel(tc, x, weights, bias, out):
                 ps = tpool.tile([P, 512], F32, tag="tp", name="pw%d_%d" % (gi, bk))
                 ta, tb = grp[2 * bk], grp[2 * bk + 1]
                 transpose_pair(ps, [(d32_of[ta[0]], ta[5]), (d32_of[tb[0]], tb[5])])
-                evacuate(nc.scalar.copy, g32[:, 512 * bk : 512 * (bk + 1)], ps)
+                evacuate(evac_engine(), g32[:, 512 * bk : 512 * (bk + 1)], ps)
             g_of[gi] = g
 
         def stage_q(gi):
@@ -249,7 +270,7 @@ def tile_locallyconnected2d_kernel(tc, x, weights, bias, out):
             if s == 3:
                 bias_broadcast()
             if s < ng:
-                ensure_s2(groups[min(s + 1, ng - 1)][-1][0])
+                ensure_s2(groups[min(s + LOOKAHEAD, ng - 1)][-1][0])
                 stage_t(s)
             if 1 <= s <= ng:
                 stage_q(s - 1)

@@ -21,15 +21,19 @@ ROW = C * NTAP
 GROUP = 4
 FLOPS = 2 * 100 * B * O * C
 
+ROW_ORDER = (1, 2, 0, 3)
+COL_ORDER = (1, 2, 0, 3)
 LOAD_BUFS = 9
-D_BUFS = 6
-G_BUFS = 3
-Q_BUFS = 4
-TP_BUFS = 5
-DUMMIES = 2
-EVAC_ACT_EVERY = 5
-LOOKAHEAD = 3
-MANUAL = True
+D_BUFS = 5
+G_BUFS = 4
+Q_BUFS = 8
+TP_BUFS = 6
+ACT_EVERY = 4
+LOOKAHEAD = 2
+STORE_CUTS = 4
+W_FIRST = 2
+X_AT = 4
+MANUAL = False
 
 
 def valid(p):
@@ -48,19 +52,34 @@ def tile_locallyconnected2d_kernel(tc, x, weights, bias, out):
         qpool = ctx.enter_context(tc.tile_pool(name="qpool", bufs=Q_BUFS))
         tpool = ctx.enter_context(tc.psum_pool(name="tpool", bufs=TP_BUFS))
         apool = ctx.enter_context(tc.psum_pool(name="apool", bufs=2))
-        spool = ctx.enter_context(tc.psum_pool(name="spool", bufs=1))
-        scratch = spool.tile([P, 512], F32, name="scratch")
 
-        locs = [(h, w) for h in range(HW) for w in range(HW)]
+        locs = [(h, w) for h in ROW_ORDER for w in COL_ORDER]
 
+        w_raw = {}
+        next_load = [0]
+
+        def load_next():
+            k = next_load[0]
+            if k < len(locs):
+                h, w = locs[k]
+                t = loads.tile([P, ROW], BF16, tag="ld", name="wraw%d" % k)
+                nc.sync.dma_start(out=t[:], in_=weights[h, w].rearrange("o c i j -> o (c i j)"))
+                w_raw[k] = t
+                next_load[0] += 1
+
+        for k in range(W_FIRST):
+            load_next()
         x_raw = []
-        for hf in range(2):
-            t = loads.tile([P, ROW], BF16, tag="ld", name="xraw%d" % hf)
+        for u in range(2):
+            t = loads.tile([P, ROW], BF16, tag="ld", name="xraw%d" % u)
             nc.sync.dma_start(
                 out=t[:, 0 : 256 * NPIX],
-                in_=x[:, 256 * hf : 256 * (hf + 1)].rearrange("b c y x -> b (c y x)"),
+                in_=x[:, 256 * u : 256 * (u + 1)].rearrange("b c y x -> b (c y x)"),
             )
             x_raw.append(t)
+        for k in range(LOAD_BUFS - 2 - W_FIRST):
+            load_next()
+
 
         ident = const.tile([P, P], F32, name="ident")
         make_identity(nc, ident[:])
@@ -74,74 +93,7 @@ def tile_locallyconnected2d_kernel(tc, x, weights, bias, out):
         xq = const.tile([P, NPIX * B], U32, name="xq", align_bytes=64)
         xs = const.tile([P, NPIX * B], U8, name="xs", align_bytes=64)
 
-        w_raw = {}
-
-        def load_w(k):
-            h, w = locs[k]
-            t = loads.tile([P, ROW], BF16, tag="ld", name="wraw%d" % k)
-            nc.sync.dma_start(out=t[:], in_=weights[h, w].rearrange("o c i j -> o (c i j)"))
-            w_raw[k] = t
-
-        next_load = [0]
-
-        def load_next():
-            if next_load[0] < len(locs):
-                load_w(next_load[0])
-                next_load[0] += 1
-
-        for k in range(LOAD_BUFS - 2):
-            load_next()
-
-        load_est = [6.5, 13.1]
-
-        def deinterleave(dst, src, n_el):
-            if load_est[0] + 0.00095 * n_el <= load_est[1] + 0.00105 * n_el:
-                load_est[0] += 0.00095 * n_el
-                nc.scalar.copy(out=dst, in_=src)
-            else:
-                load_est[1] += 0.00105 * n_el
-                nc.gpsimd.tensor_scalar(
-                    out=dst, in0=src, scalar1=1.0, scalar2=0.0, op0=mybir.AluOpType.mult, op1=mybir.AluOpType.add
-                )
-
-        n_evac = [0]
-
-        def evac_engine():
-            n_evac[0] += 1
-            return nc.scalar.copy if n_evac[0] % EVAC_ACT_EVERY == 0 else nc.vector.tensor_copy
-
-        def transpose_pair(ps, slots):
-            for t in range(2):
-                d, s = slots[t]
-                for u in range(2):
-                    nc.tensor.transpose(
-                        ps[:, (2 * t + u) * P : (2 * t + u + 1) * P],
-                        d[:, s * 256 + u * P : s * 256 + (u + 1) * P],
-                        ident[:],
-                    )
-
-        def evacuate(engine_copy, g32, ps):
-            engine_copy(
-                out=g32.rearrange("p (t o u) -> p t o u", t=2, u=2),
-                in_=ps[:].rearrange("p (t u o) -> p t o u", t=2, u=2),
-            )
-
-        dxs = [dpool.tile([P, ROW], BF16, tag="d", name="dx%d" % pg) for pg in range(2)]
-        n_x = 0
-        for hf in range(2):
-            for pg in range(2):
-                for q4 in range(2):
-                    n_x += 1
-                    (nc.scalar.copy if n_x % 3 == 2 else nc.vector.tensor_copy)(
-                        out=dxs[pg][:, 0 : 8 * C].rearrange("b (s c) -> b c s", c=C)[
-                            :, 256 * hf : 256 * (hf + 1), 4 * q4 : 4 * q4 + 4
-                        ],
-                        in_=x_raw[hf][:, 0 : 256 * NPIX].rearrange("b (c s) -> b c s", s=NPIX)[
-                            :, :, 8 * pg + 4 * q4 : 8 * pg + 4 * q4 + 4
-                        ],
-                    )
-        load_next()
-        load_next()
+        x32 = [x_raw[u][:, 0 : 256 * NPIX].bitcast(F32) for u in range(2)]
         pending = []
         n_xq = [0]
 
@@ -154,24 +106,31 @@ def tile_locallyconnected2d_kernel(tc, x, weights, bias, out):
                 in_=g[:],
             )
 
-        for pg in range(2):
-            dx32 = dxs[pg][:].bitcast(F32)
-            for half in range(2):
-                g = gpool.tile([P, GROUP * C], BF16, tag="g", name="gx%d_%d" % (pg, half), align_bytes=64)
-                g32 = g[:].bitcast(F32)
+        def x_phase():
+            for quad in range(4):
+                g = gpool.tile([P, GROUP * C], BF16, tag="g", name="gx%d" % quad, align_bytes=64)
                 for bk in range(2):
-                    ps = tpool.tile([P, 512], F32, tag="tp", name="px%d_%d_%d" % (pg, half, bk))
-                    s0 = 4 * half + 2 * bk
-                    transpose_pair(ps, [(dx32, s0), (dx32, s0 + 1)])
-                    evacuate(
-                        nc.scalar.copy if bk == 0 else nc.vector.tensor_copy,
-                        g32[:, 512 * bk : 512 * (bk + 1)],
-                        ps,
+                    rho = 2 * quad + bk
+                    ps = tpool.tile([P, 512], F32, tag="tp", name="px%d" % rho)
+                    for u in range(2):
+                        for par in range(2):
+                            j = 2 * u + par
+                            first = 8 * par + rho
+                            nc.tensor.transpose(
+                                ps[:, j * P : (j + 1) * P],
+                                x32[u][:, first : first + 16 * (P - 1) + 1 : 16],
+                                ident[:],
+                            )
+                    (nc.scalar.copy if bk == 0 else nc.vector.tensor_copy)(
+                        out=g[:, 1024 * bk : 1024 * (bk + 1)].rearrange("p (e b j) -> p e b j", e=2, j=4),
+                        in_=ps[:].bitcast(BF16).rearrange("p (j b e) -> p e b j", j=4, e=2),
                     )
-                pending.append((g, (8 * pg + 4 * half) * B))
+                pending.append((g, quad * GROUP * B))
                 if len(pending) > 1:
                     quantise_x()
-        quantise_x()
+            quantise_x()
+            load_next()
+            load_next()
 
         taps = []
         for k, (h, w) in enumerate(locs):
@@ -180,6 +139,15 @@ def tile_locallyconnected2d_kernel(tc, x, weights, bias, out):
                 taps.append((k, h, w, i, j, s, s == 0, s == len(lst) - 1))
         groups = [taps[a : a + GROUP] for a in range(0, len(taps), GROUP)]
         ng = len(groups)
+
+        counter = [1]
+
+        def deinterleave(dst, src):
+            counter[0] += 1
+            if counter[0] % ACT_EVERY == 0:
+                nc.scalar.copy(out=dst, in_=src)
+            else:
+                nc.vector.tensor_copy(out=dst, in_=src)
 
         d32_of = {}
 
@@ -193,7 +161,6 @@ def tile_locallyconnected2d_kernel(tc, x, weights, bias, out):
                 deinterleave(
                     d[:, a * nj * C : (a + 1) * nj * C].rearrange("o (s c) -> o c s", c=C),
                     src[:, :, KK * i + js[0] : KK * i + js[0] + nj],
-                    nj * C,
                 )
             load_next()
             d32_of[k] = d[:].bitcast(F32)
@@ -215,9 +182,19 @@ def tile_locallyconnected2d_kernel(tc, x, weights, bias, out):
             g32 = g[:].bitcast(F32)
             for bk in range(2):
                 ps = tpool.tile([P, 512], F32, tag="tp", name="pw%d_%d" % (gi, bk))
-                ta, tb = grp[2 * bk], grp[2 * bk + 1]
-                transpose_pair(ps, [(d32_of[ta[0]], ta[5]), (d32_of[tb[0]], tb[5])])
-                evacuate(evac_engine(), g32[:, 512 * bk : 512 * (bk + 1)], ps)
+                for t in range(2):
+                    tap = grp[2 * bk + t]
+                    d32 = d32_of[tap[0]]
+                    for u in range(2):
+                        nc.tensor.transpose(
+                            ps[:, (2 * t + u) * P : (2 * t + u + 1) * P],
+                            d32[:, tap[5] * 256 + u * P : tap[5] * 256 + (u + 1) * P],
+                            ident[:],
+                        )
+                nc.scalar.copy(
+                    out=g32[:, 512 * bk : 512 * (bk + 1)].rearrange("p (t o u) -> p t o u", t=2, u=2),
+                    in_=ps[:].rearrange("p (t u o) -> p t o u", t=2, u=2),
+                )
             g_of[gi] = g
 
         def stage_q(gi):
@@ -226,20 +203,31 @@ def tile_locallyconnected2d_kernel(tc, x, weights, bias, out):
             nc.vector.quantize_mx(out=wq[:].bitcast(FP8X4), scales=ws[:], in_=g_of[gi][:])
             q_of[gi] = (wq, ws)
 
+        res3 = result[:].rearrange("b (o l) -> b o l", l=NPIX)
+        bias3 = bias_all[:].rearrange("b (o l) -> b o l", l=NPIX)
+        out2 = out.rearrange("b o y x -> b (o y x)")
+
+        def finish_row(h, acc):
+            acc3 = acc[:].rearrange("b (w o) -> b o w", w=HW)
+            cuts = STORE_CUTS if h == ROW_ORDER[-1] else 1
+            step = O // cuts
+            for q in range(cuts):
+                nc.vector.tensor_tensor(
+                    out=res3[:, q * step : (q + 1) * step, HW * h : HW * (h + 1)],
+                    in0=acc3[:, q * step : (q + 1) * step, :],
+                    in1=bias3[:, q * step : (q + 1) * step, HW * h : HW * (h + 1)],
+                    op=mybir.AluOpType.add,
+                )
+                if h == ROW_ORDER[-1]:
+                    nc.sync.dma_start(
+                        out=out2[:, q * step * NPIX : (q + 1) * step * NPIX],
+                        in_=result[:, q * step * NPIX : (q + 1) * step * NPIX],
+                    )
+
         def stage_m(gi):
             wq, ws = q_of[gi]
-            for n in range(DUMMIES):
-                nc.tensor.matmul_mx(
-                    out=scratch[:],
-                    lhsT=xq[:, 0:B].bitcast(FP8X4),
-                    lhsT_scale=xs[:, 0:B],
-                    rhs=wq[:].bitcast(FP8X4),
-                    rhs_scale=ws[:],
-                    start=True,
-                    stop=True,
-                )
             for n, (k, h, w, i, j, s, first, last) in enumerate(groups[gi]):
-                if w == 0 and first:
+                if w == COL_ORDER[0] and first:
                     acc_of[h] = apool.tile([P, 512], F32, tag="acc", name="acc%d" % h)
                 acc = acc_of[h]
                 pix = (h + i - 1) * HW + (w + j - 1)
@@ -252,13 +240,8 @@ def tile_locallyconnected2d_kernel(tc, x, weights, bias, out):
                     start=first,
                     stop=last,
                 )
-                if w == HW - 1 and last:
-                    nc.vector.tensor_tensor(
-                        out=result[:].rearrange("b (o l) -> b o l", l=NPIX)[:, :, HW * h : HW * (h + 1)],
-                        in0=acc[:].rearrange("b (w o) -> b o w", w=HW),
-                        in1=bias_all[:].rearrange("b (o l) -> b o l", l=NPIX)[:, :, HW * h : HW * (h + 1)],
-                        op=mybir.AluOpType.add,
-                    )
+                if w == COL_ORDER[-1] and last:
+                    finish_row(h, acc)
 
         def bias_broadcast():
             for k in range(4):
@@ -266,15 +249,17 @@ def tile_locallyconnected2d_kernel(tc, x, weights, bias, out):
                 nc.tensor.matmul(pb[:], lhsT=ones[:], rhs=brow[:, 512 * k : 512 * (k + 1)], start=True, stop=True)
                 nc.scalar.copy(out=bias_all[:, 512 * k : 512 * (k + 1)], in_=pb[:])
 
+        m_done = [0]
         for s in range(ng + 2):
-            if s == 3:
+            if s == X_AT:
+                x_phase()
+            if s == X_AT + 2:
                 bias_broadcast()
             if s < ng:
-                ensure_s2(groups[min(s + LOOKAHEAD, ng - 1)][-1][0])
+                ensure_s2(W_FIRST - 1 if s < X_AT else groups[min(s + LOOKAHEAD, ng - 1)][-1][0])
                 stage_t(s)
             if 1 <= s <= ng:
                 stage_q(s - 1)
-            if s >= 2:
-                stage_m(s - 2)
-
-        nc.sync.dma_start(out=out.rearrange("b o y x -> b (o y x)"), in_=result[:])
+            while s >= X_AT and m_done[0] <= s - 2:
+                stage_m(m_done[0])
+                m_done[0] += 1

@@ -18,21 +18,23 @@ KK = 3
 NPIX = HW * HW
 NTAP = KK * KK
 ROW = C * NTAP
-GROUP = 4
+GROUP = 8
+XGROUP = 4
 FLOPS = 2 * 100 * B * O * C
 
 ROW_ORDER = (1, 2, 0, 3)
 COL_ORDER = (1, 2, 0, 3)
 LOAD_BUFS = 9
 D_BUFS = 5
-G_BUFS = 4
-Q_BUFS = 8
+G_BUFS = 3
+Q_BUFS = 5
 TP_BUFS = 6
 ACT_EVERY = 4
-LOOKAHEAD = 2
+LOOKAHEAD = 1
 STORE_CUTS = 4
 W_FIRST = 2
-X_AT = 4
+X_AT = 2
+X_ON_VECTOR = (1, 3, 5, 7)
 MANUAL = False
 
 
@@ -63,7 +65,15 @@ def tile_locallyconnected2d_kernel(tc, x, weights, bias, out):
             if k < len(locs):
                 h, w = locs[k]
                 t = loads.tile([P, ROW], BF16, tag="ld", name="wraw%d" % k)
-                nc.sync.dma_start(out=t[:], in_=weights[h, w].rearrange("o c i j -> o (c i j)"))
+                rows = weights[h, w].rearrange("o c i j -> o (c i j)")
+                if k == 0:
+                    for half in range(2):
+                        nc.sync.dma_start(
+                            out=t[:, half * ROW // 2 : (half + 1) * ROW // 2],
+                            in_=rows[:, half * ROW // 2 : (half + 1) * ROW // 2],
+                        )
+                else:
+                    nc.sync.dma_start(out=t[:], in_=rows)
                 w_raw[k] = t
                 next_load[0] += 1
 
@@ -83,12 +93,8 @@ def tile_locallyconnected2d_kernel(tc, x, weights, bias, out):
 
         ident = const.tile([P, P], F32, name="ident")
         make_identity(nc, ident[:])
-        ones = const.tile([P, P], BF16, name="ones")
-        nc.vector.memset(ones[:], 1.0)
-        brow = const.tile([P, O * NPIX], BF16, name="brow")
-        nc.vector.memset(brow[:], 0.0)
-        nc.scalar.dma_start(out=brow[0:1, :], in_=bias.rearrange("(a o) y x -> a (o y x)", a=1))
-        bias_all = const.tile([P, O * NPIX], F32, name="bias_all")
+        bias_all = const.tile([P, O * NPIX], BF16, name="bias_all")
+        nc.sync.dma_start(out=bias_all[:], in_=bias.rearrange("o y x -> (o y x)").partition_broadcast(P))
         result = const.tile([P, O * NPIX], F32, name="result")
         xq = const.tile([P, NPIX * B], U32, name="xq", align_bytes=64)
         xs = const.tile([P, NPIX * B], U8, name="xs", align_bytes=64)
@@ -101,14 +107,14 @@ def tile_locallyconnected2d_kernel(tc, x, weights, bias, out):
             g, p0 = pending[n_xq[0]]
             n_xq[0] += 1
             nc.vector.quantize_mx(
-                out=xq[:, p0 : p0 + GROUP * B].bitcast(FP8X4),
-                scales=xs[:, p0 : p0 + GROUP * B],
+                out=xq[:, p0 : p0 + XGROUP * B].bitcast(FP8X4),
+                scales=xs[:, p0 : p0 + XGROUP * B],
                 in_=g[:],
             )
 
         def x_phase():
             for quad in range(4):
-                g = gpool.tile([P, GROUP * C], BF16, tag="g", name="gx%d" % quad, align_bytes=64)
+                g = gpool.tile([P, XGROUP * C], BF16, tag="g", name="gx%d" % quad, align_bytes=64)
                 for bk in range(2):
                     rho = 2 * quad + bk
                     ps = tpool.tile([P, 512], F32, tag="tp", name="px%d" % rho)
@@ -121,11 +127,11 @@ def tile_locallyconnected2d_kernel(tc, x, weights, bias, out):
                                 x32[u][:, first : first + 16 * (P - 1) + 1 : 16],
                                 ident[:],
                             )
-                    (nc.scalar.copy if bk == 0 else nc.vector.tensor_copy)(
+                    (nc.vector.tensor_copy if rho in X_ON_VECTOR else nc.scalar.copy)(
                         out=g[:, 1024 * bk : 1024 * (bk + 1)].rearrange("p (e b j) -> p e b j", e=2, j=4),
                         in_=ps[:].bitcast(BF16).rearrange("p (j b e) -> p e b j", j=4, e=2),
                     )
-                pending.append((g, quad * GROUP * B))
+                pending.append((g, quad * XGROUP * B))
                 if len(pending) > 1:
                     quantise_x()
             quantise_x()
@@ -137,10 +143,12 @@ def tile_locallyconnected2d_kernel(tc, x, weights, bias, out):
             lst = [(i, j) for i in valid(h) for j in valid(w)]
             for s, (i, j) in enumerate(lst):
                 taps.append((k, h, w, i, j, s, s == 0, s == len(lst) - 1))
-        groups = [taps[a : a + GROUP] for a in range(0, len(taps), GROUP)]
+        n_coarse = 80
+        groups = [taps[a : a + GROUP] for a in range(0, n_coarse, GROUP)]
+        groups += [taps[a : a + XGROUP] for a in range(n_coarse, len(taps), XGROUP)]
         ng = len(groups)
 
-        counter = [1]
+        counter = [0]
 
         def deinterleave(dst, src):
             counter[0] += 1
@@ -154,14 +162,33 @@ def tile_locallyconnected2d_kernel(tc, x, weights, bias, out):
         def s2(k):
             h, w = locs[k]
             js = valid(w)
+            rows_i = valid(h)
             nj = len(js)
             d = dpool.tile([P, ROW], BF16, tag="d", name="d%d" % k)
-            src = w_raw[k][:].rearrange("o (c t) -> o c t", t=NTAP)
-            for a, i in enumerate(valid(h)):
-                deinterleave(
-                    d[:, a * nj * C : (a + 1) * nj * C].rearrange("o (s c) -> o c s", c=C),
-                    src[:, :, KK * i + js[0] : KK * i + js[0] + nj],
-                )
+            src = w_raw[k][:].rearrange("o (c i j) -> o c i j", i=KK, j=KK)
+            if k == 0:
+                for half in range(2):
+                    cs = slice(half * C // 2, (half + 1) * C // 2)
+                    for a, i in enumerate(rows_i):
+                        (nc.scalar.copy if a == 1 else nc.vector.tensor_copy)(
+                            out=d[:, a * nj * C : (a + 1) * nj * C].rearrange("o (s c) -> o c s", c=C)[:, cs, :],
+                            in_=src[:, cs, i, js[0] : js[0] + nj],
+                        )
+            else:
+                a = 0
+                while a < len(rows_i):
+                    ni = 2 if (nj == 2 and a + 1 < len(rows_i)) else 1
+                    if ni == 2:
+                        deinterleave(
+                            d[:, a * nj * C : (a + 2) * nj * C].rearrange("o (i j c) -> o c i j", i=2, j=2),
+                            src[:, :, rows_i[a] : rows_i[a] + 2, js[0] : js[0] + 2],
+                        )
+                    else:
+                        deinterleave(
+                            d[:, a * nj * C : (a + 1) * nj * C].rearrange("o (s c) -> o c s", c=C),
+                            src[:, :, rows_i[a], js[0] : js[0] + nj],
+                        )
+                    a += ni
             load_next()
             d32_of[k] = d[:].bitcast(F32)
 
@@ -180,7 +207,7 @@ def tile_locallyconnected2d_kernel(tc, x, weights, bias, out):
             grp = groups[gi]
             g = gpool.tile([P, GROUP * C], BF16, tag="g", name="g%d" % gi, align_bytes=64)
             g32 = g[:].bitcast(F32)
-            for bk in range(2):
+            for bk in range(len(grp) // 2):
                 ps = tpool.tile([P, 512], F32, tag="tp", name="pw%d_%d" % (gi, bk))
                 for t in range(2):
                     tap = grp[2 * bk + t]
@@ -200,7 +227,10 @@ def tile_locallyconnected2d_kernel(tc, x, weights, bias, out):
         def stage_q(gi):
             wq = qpool.tile([P, GROUP * O], U32, tag="wq", name="wq%d" % gi, align_bytes=64)
             ws = qpool.tile([P, GROUP * O], U8, tag="ws", name="ws%d" % gi, align_bytes=64)
-            nc.vector.quantize_mx(out=wq[:].bitcast(FP8X4), scales=ws[:], in_=g_of[gi][:])
+            n = len(groups[gi])
+            nc.vector.quantize_mx(
+                out=wq[:, 0 : n * O].bitcast(FP8X4), scales=ws[:, 0 : n * O], in_=g_of[gi][:, 0 : n * C]
+            )
             q_of[gi] = (wq, ws)
 
         res3 = result[:].rearrange("b (o l) -> b o l", l=NPIX)
@@ -243,18 +273,10 @@ def tile_locallyconnected2d_kernel(tc, x, weights, bias, out):
                 if w == COL_ORDER[-1] and last:
                     finish_row(h, acc)
 
-        def bias_broadcast():
-            for k in range(4):
-                pb = tpool.tile([P, 512], F32, tag="tp", name="pb%d" % k)
-                nc.tensor.matmul(pb[:], lhsT=ones[:], rhs=brow[:, 512 * k : 512 * (k + 1)], start=True, stop=True)
-                nc.scalar.copy(out=bias_all[:, 512 * k : 512 * (k + 1)], in_=pb[:])
-
         m_done = [0]
         for s in range(ng + 2):
             if s == X_AT:
                 x_phase()
-            if s == X_AT + 2:
-                bias_broadcast()
             if s < ng:
                 ensure_s2(W_FIRST - 1 if s < X_AT else groups[min(s + LOOKAHEAD, ng - 1)][-1][0])
                 stage_t(s)

@@ -18,7 +18,7 @@ KK = 3
 NPIX = HW * HW
 NTAP = KK * KK
 ROW = C * NTAP
-GROUP = 8
+GROUP = 4
 XGROUP = 4
 FLOPS = 2 * 100 * B * O * C
 
@@ -26,14 +26,15 @@ ROW_ORDER = (1, 2, 0, 3)
 COL_ORDER = (1, 2, 0, 3)
 LOAD_BUFS = 9
 D_BUFS = 5
-G_BUFS = 3
-Q_BUFS = 5
-TP_BUFS = 6
+G_BUFS = 4
+Q_BUFS = 8
+TP_BUFS = 5
+DUMMIES = 2
 ACT_EVERY = 4
-LOOKAHEAD = 1
+LOOKAHEAD = 2
 STORE_CUTS = 4
 W_FIRST = 2
-X_AT = 2
+X_AT = 4
 X_ON_VECTOR = (1, 3, 5, 7)
 MANUAL = False
 
@@ -54,6 +55,8 @@ def tile_locallyconnected2d_kernel(tc, x, weights, bias, out):
         qpool = ctx.enter_context(tc.tile_pool(name="qpool", bufs=Q_BUFS))
         tpool = ctx.enter_context(tc.psum_pool(name="tpool", bufs=TP_BUFS))
         apool = ctx.enter_context(tc.psum_pool(name="apool", bufs=2))
+        spool = ctx.enter_context(tc.psum_pool(name="spool", bufs=1))
+        scratch = spool.tile([P, 512], F32, name="scratch")
 
         locs = [(h, w) for h in ROW_ORDER for w in COL_ORDER]
 
@@ -256,6 +259,16 @@ def tile_locallyconnected2d_kernel(tc, x, weights, bias, out):
 
         def stage_m(gi):
             wq, ws = q_of[gi]
+            for n in range(DUMMIES):
+                nc.tensor.matmul_mx(
+                    out=scratch[:],
+                    lhsT=xq[:, 0:B].bitcast(FP8X4),
+                    lhsT_scale=xs[:, 0:B],
+                    rhs=wq[:].bitcast(FP8X4),
+                    rhs_scale=ws[:],
+                    start=True,
+                    stop=True,
+                )
             for n, (k, h, w, i, j, s, first, last) in enumerate(groups[gi]):
                 if w == COL_ORDER[0] and first:
                     acc_of[h] = apool.tile([P, 512], F32, tag="acc", name="acc%d" % h)

@@ -18,7 +18,7 @@ KK = 3
 NPIX = HW * HW
 NTAP = KK * KK
 ROW = C * NTAP
-GROUP = 4
+GROUP = 8
 XGROUP = 4
 FLOPS = 2 * 100 * B * O * C
 
@@ -26,17 +26,16 @@ ROW_ORDER = (1, 2, 0, 3)
 COL_ORDER = (1, 2, 0, 3)
 LOAD_BUFS = 9
 D_BUFS = 5
-G_BUFS = 4
-Q_BUFS = 8
-TP_BUFS = 5
-DUMMIES = 2
+G_BUFS = 3
+Q_BUFS = 5
+TP_BUFS = 6
 ACT_EVERY = 4
-LOOKAHEAD = 2
+LOOKAHEAD = 1
 STORE_CUTS = 4
 W_FIRST = 2
-X_AT = 4
+X_AT = 2
 X_ON_VECTOR = (1, 3, 5, 7)
-MANUAL = False
+MANUAL = True
 
 
 def valid(p):
@@ -55,8 +54,6 @@ def tile_locallyconnected2d_kernel(tc, x, weights, bias, out):
         qpool = ctx.enter_context(tc.tile_pool(name="qpool", bufs=Q_BUFS))
         tpool = ctx.enter_context(tc.psum_pool(name="tpool", bufs=TP_BUFS))
         apool = ctx.enter_context(tc.psum_pool(name="apool", bufs=2))
-        spool = ctx.enter_context(tc.psum_pool(name="spool", bufs=1))
-        scratch = spool.tile([P, 512], F32, name="scratch")
 
         locs = [(h, w) for h in ROW_ORDER for w in COL_ORDER]
 
@@ -259,16 +256,6 @@ def tile_locallyconnected2d_kernel(tc, x, weights, bias, out):
 
         def stage_m(gi):
             wq, ws = q_of[gi]
-            for n in range(DUMMIES):
-                nc.tensor.matmul_mx(
-                    out=scratch[:],
-                    lhsT=xq[:, 0:B].bitcast(FP8X4),
-                    lhsT_scale=xs[:, 0:B],
-                    rhs=wq[:].bitcast(FP8X4),
-                    rhs_scale=ws[:],
-                    start=True,
-                    stop=True,
-                )
             for n, (k, h, w, i, j, s, first, last) in enumerate(groups[gi]):
                 if w == COL_ORDER[0] and first:
                     acc_of[h] = apool.tile([P, 512], F32, tag="acc", name="acc%d" % h)

@@ -34,7 +34,7 @@ LOOKAHEAD = 1
 STORE_CUTS = 4
 W_FIRST = 2
 X_AT = 2
-X_ON_VECTOR = (1, 3, 5, 7)
+X_ON_VECTOR = (3, 7)
 MANUAL = True
 
 
@@ -134,6 +134,8 @@ def tile_locallyconnected2d_kernel(tc, x, weights, bias, out):
                 pending.append((g, quad * XGROUP * B))
                 if len(pending) > 1:
                     quantise_x()
+                if quad == 1:
+                    ensure_s2(W_FIRST)
             quantise_x()
             load_next()
             load_next()
@@ -148,7 +150,7 @@ def tile_locallyconnected2d_kernel(tc, x, weights, bias, out):
         groups += [taps[a : a + XGROUP] for a in range(n_coarse, len(taps), XGROUP)]
         ng = len(groups)
 
-        counter = [0]
+        counter = [1]
 
         def deinterleave(dst, src):
             counter[0] += 1

from contextlib import ExitStack

import concourse.mybir as mybir
from concourse.masks import make_identity

BF16 = mybir.dt.bfloat16
F32 = mybir.dt.float32
U32 = mybir.dt.uint32
U8 = mybir.dt.uint8
FP8X4 = mybir.dt.float8_e4m3fn_x4

P = 128
B = 128
C = 512
O = 128
HW = 4
KK = 3
NPIX = HW * HW
NTAP = KK * KK
ROW = C * NTAP
GROUP = 8
XGROUP = 4
FLOPS = 2 * 100 * B * O * C

ROW_ORDER = (1, 2, 0, 3)
COL_ORDER = (1, 2, 0, 3)
LOAD_BUFS = 9
D_BUFS = 5
G_BUFS = 3
Q_BUFS = 5
TP_BUFS = 6
ACT_EVERY = 4
LOOKAHEAD = 1
STORE_CUTS = 4
W_FIRST = 2
X_AT = 2
X_ON_VECTOR = (3, 7)
MANUAL = True


def valid(p):
    return [t for t in range(KK) if 0 <= p + t - 1 < HW]


def tile_locallyconnected2d_kernel(tc, x, weights, bias, out):
    nc = tc.nc
    with ExitStack() as ctx:
        if MANUAL:
            ctx.enter_context(tc.manual_schedule())
        const = ctx.enter_context(tc.tile_pool(name="const", bufs=1))
        loads = ctx.enter_context(tc.tile_pool(name="loads", bufs=LOAD_BUFS))
        dpool = ctx.enter_context(tc.tile_pool(name="dpool", bufs=D_BUFS))
        gpool = ctx.enter_context(tc.tile_pool(name="gpool", bufs=G_BUFS))
        qpool = ctx.enter_context(tc.tile_pool(name="qpool", bufs=Q_BUFS))
        tpool = ctx.enter_context(tc.psum_pool(name="tpool", bufs=TP_BUFS))
        apool = ctx.enter_context(tc.psum_pool(name="apool", bufs=2))

        locs = [(h, w) for h in ROW_ORDER for w in COL_ORDER]

        w_raw = {}
        next_load = [0]

        def load_next():
            k = next_load[0]
            if k < len(locs):
                h, w = locs[k]
                t = loads.tile([P, ROW], BF16, tag="ld", name="wraw%d" % k)
                rows = weights[h, w].rearrange("o c i j -> o (c i j)")
                if k == 0:
                    for half in range(2):
                        nc.sync.dma_start(
                            out=t[:, half * ROW // 2 : (half + 1) * ROW // 2],
                            in_=rows[:, half * ROW // 2 : (half + 1) * ROW // 2],
                        )
                else:
                    nc.sync.dma_start(out=t[:], in_=rows)
                w_raw[k] = t
                next_load[0] += 1

        for k in range(W_FIRST):
            load_next()
        x_raw = []
        for u in range(2):
            t = loads.tile([P, ROW], BF16, tag="ld", name="xraw%d" % u)
            nc.sync.dma_start(
                out=t[:, 0 : 256 * NPIX],
                in_=x[:, 256 * u : 256 * (u + 1)].rearrange("b c y x -> b (c y x)"),
            )
            x_raw.append(t)
        for k in range(LOAD_BUFS - 2 - W_FIRST):
            load_next()


        ident = const.tile([P, P], F32, name="ident")
        make_identity(nc, ident[:])
        bias_all = const.tile([P, O * NPIX], BF16, name="bias_all")
        nc.sync.dma_start(out=bias_all[:], in_=bias.rearrange("o y x -> (o y x)").partition_broadcast(P))
        result = const.tile([P, O * NPIX], F32, name="result")
        xq = const.tile([P, NPIX * B], U32, name="xq", align_bytes=64)
        xs = const.tile([P, NPIX * B], U8, name="xs", align_bytes=64)

        x32 = [x_raw[u][:, 0 : 256 * NPIX].bitcast(F32) for u in range(2)]
        pending = []
        n_xq = [0]

        def quantise_x():
            g, p0 = pending[n_xq[0]]
            n_xq[0] += 1
            nc.vector.quantize_mx(
                out=xq[:, p0 : p0 + XGROUP * B].bitcast(FP8X4),
                scales=xs[:, p0 : p0 + XGROUP * B],
                in_=g[:],
            )

        def x_phase():
            for quad in range(4):
                g = gpool.tile([P, XGROUP * C], BF16, tag="g", name="gx%d" % quad, align_bytes=64)
                for bk in range(2):
                    rho = 2 * quad + bk
                    ps = tpool.tile([P, 512], F32, tag="tp", name="px%d" % rho)
                    for u in range(2):
                        for par in range(2):
                            j = 2 * u + par
                            first = 8 * par + rho
                            nc.tensor.transpose(
                                ps[:, j * P : (j + 1) * P],
                                x32[u][:, first : first + 16 * (P - 1) + 1 : 16],
                                ident[:],
                            )
                    (nc.vector.tensor_copy if rho in X_ON_VECTOR else nc.scalar.copy)(
                        out=g[:, 1024 * bk : 1024 * (bk + 1)].rearrange("p (e b j) -> p e b j", e=2, j=4),
                        in_=ps[:].bitcast(BF16).rearrange("p (j b e) -> p e b j", j=4, e=2),
                    )
                pending.append((g, quad * XGROUP * B))
                if len(pending) > 1:
                    quantise_x()
                if quad == 1:
                    ensure_s2(W_FIRST)
            quantise_x()
            load_next()
            load_next()

        taps = []
        for k, (h, w) in enumerate(locs):
            lst = [(i, j) for i in valid(h) for j in valid(w)]
            for s, (i, j) in enumerate(lst):
                taps.append((k, h, w, i, j, s, s == 0, s == len(lst) - 1))
        n_coarse = 80
        groups = [taps[a : a + GROUP] for a in range(0, n_coarse, GROUP)]
        groups += [taps[a : a + XGROUP] for a in range(n_coarse, len(taps), XGROUP)]
        ng = len(groups)

        counter = [1]

        def deinterleave(dst, src):
            counter[0] += 1
            if counter[0] % ACT_EVERY == 0:
                nc.scalar.copy(out=dst, in_=src)
            else:
                nc.vector.tensor_copy(out=dst, in_=src)

        d32_of = {}

        def s2(k):
            h, w = locs[k]
            js = valid(w)
            rows_i = valid(h)
            nj = len(js)
            d = dpool.tile([P, ROW], BF16, tag="d", name="d%d" % k)
            src = w_raw[k][:].rearrange("o (c i j) -> o c i j", i=KK, j=KK)
            if k == 0:
                for half in range(2):
                    cs = slice(half * C // 2, (half + 1) * C // 2)
                    for a, i in enumerate(rows_i):
                        (nc.scalar.copy if a == 1 else nc.vector.tensor_copy)(
                            out=d[:, a * nj * C : (a + 1) * nj * C].rearrange("o (s c) -> o c s", c=C)[:, cs, :],
                            in_=src[:, cs, i, js[0] : js[0] + nj],
                        )
            else:
                a = 0
                while a < len(rows_i):
                    ni = 2 if (nj == 2 and a + 1 < len(rows_i)) else 1
                    if ni == 2:
                        deinterleave(
                            d[:, a * nj * C : (a + 2) * nj * C].rearrange("o (i j c) -> o c i j", i=2, j=2),
                            src[:, :, rows_i[a] : rows_i[a] + 2, js[0] : js[0] + 2],
                        )
                    else:
                        deinterleave(
                            d[:, a * nj * C : (a + 1) * nj * C].rearrange("o (s c) -> o c s", c=C),
                            src[:, :, rows_i[a], js[0] : js[0] + nj],
                        )
                    a += ni
            load_next()
            d32_of[k] = d[:].bitcast(F32)

        done_s2 = [0]

        def ensure_s2(upto):
            while done_s2[0] <= upto:
                s2(done_s2[0])
                done_s2[0] += 1

        g_of = {}
        q_of = {}
        acc_of = {}

        def stage_t(gi):
            grp = groups[gi]
            g = gpool.tile([P, GROUP * C], BF16, tag="g", name="g%d" % gi, align_bytes=64)
            g32 = g[:].bitcast(F32)
            for bk in range(len(grp) // 2):
                ps = tpool.tile([P, 512], F32, tag="tp", name="pw%d_%d" % (gi, bk))
                for t in range(2):
                    tap = grp[2 * bk + t]
                    d32 = d32_of[tap[0]]
                    for u in range(2):
                        nc.tensor.transpose(
                            ps[:, (2 * t + u) * P : (2 * t + u + 1) * P],
                            d32[:, tap[5] * 256 + u * P : tap[5] * 256 + (u + 1) * P],
                            ident[:],
                        )
                nc.scalar.copy(
                    out=g32[:, 512 * bk : 512 * (bk + 1)].rearrange("p (t o u) -> p t o u", t=2, u=2),
                    in_=ps[:].rearrange("p (t u o) -> p t o u", t=2, u=2),
                )
            g_of[gi] = g

        def stage_q(gi):
            wq = qpool.tile([P, GROUP * O], U32, tag="wq", name="wq%d" % gi, align_bytes=64)
            ws = qpool.tile([P, GROUP * O], U8, tag="ws", name="ws%d" % gi, align_bytes=64)
            n = len(groups[gi])
            nc.vector.quantize_mx(
                out=wq[:, 0 : n * O].bitcast(FP8X4), scales=ws[:, 0 : n * O], in_=g_of[gi][:, 0 : n * C]
            )
            q_of[gi] = (wq, ws)

        res3 = result[:].rearrange("b (o l) -> b o l", l=NPIX)
        bias3 = bias_all[:].rearrange("b (o l) -> b o l", l=NPIX)
        out2 = out.rearrange("b o y x -> b (o y x)")

        def finish_row(h, acc):
            acc3 = acc[:].rearrange("b (w o) -> b o w", w=HW)
            cuts = STORE_CUTS if h == ROW_ORDER[-1] else 1
            step = O // cuts
            for q in range(cuts):
                nc.vector.tensor_tensor(
                    out=res3[:, q * step : (q + 1) * step, HW * h : HW * (h + 1)],
                    in0=acc3[:, q * step : (q + 1) * step, :],
                    in1=bias3[:, q * step : (q + 1) * step, HW * h : HW * (h + 1)],
                    op=mybir.AluOpType.add,
                )
                if h == ROW_ORDER[-1]:
                    nc.sync.dma_start(
                        out=out2[:, q * step * NPIX : (q + 1) * step * NPIX],
                        in_=result[:, q * step * NPIX : (q + 1) * step * NPIX],
                    )

        def stage_m(gi):
            wq, ws = q_of[gi]
            for n, (k, h, w, i, j, s, first, last) in enumerate(groups[gi]):
                if w == COL_ORDER[0] and first:
                    acc_of[h] = apool.tile([P, 512], F32, tag="acc", name="acc%d" % h)
                acc = acc_of[h]
                pix = (h + i - 1) * HW + (w + j - 1)
                nc.tensor.matmul_mx(
                    out=acc[:, w * O : (w + 1) * O],
                    lhsT=xq[:, pix * B : (pix + 1) * B].bitcast(FP8X4),
                    lhsT_scale=xs[:, pix * B : (pix + 1) * B],
                    rhs=wq[:, n * O : (n + 1) * O].bitcast(FP8X4),
                    rhs_scale=ws[:, n * O : (n + 1) * O],
                    start=first,
                    stop=last,
                )
                if w == COL_ORDER[-1] and last:
                    finish_row(h, acc)

        m_done = [0]
        for s in range(ng + 2):
            if s == X_AT:
                x_phase()
            if s < ng:
                ensure_s2(W_FIRST - 1 if s < X_AT else groups[min(s + LOOKAHEAD, ng - 1)][-1][0])
                stage_t(s)
            if 1 <= s <= ng:
                stage_q(s - 1)
            while s >= X_AT and m_done[0] <= s - 2:
                stage_m(m_done[0])
                m_done[0] += 1
